import numpy as np
import ml_dtypes

BF16 = ml_dtypes.bfloat16


def bf(x):
    return np.asarray(x, np.float32).astype(BF16)


def f32(x):
    return np.asarray(x, np.float32)


def f64(x):
    return np.asarray(x).astype(np.float64)


def striped(idx):
    return np.tile(idx.reshape(-1, 16).T, (8, 1))


D, K, S, P, N = 128, 64, 2048, 512, 1536


def rot(theta, v):
    c, s = np.cos(theta), np.sin(theta)
    return np.concatenate([c * v[:K] - s * v[K:], s * v[:K] + c * v[K:]], axis=0)


def setup_inputs():
    return {"table": bf(np.random.standard_normal((D, S))), "w": bf(np.random.standard_normal((D, D)) / np.sqrt(D)), "b": f32(0.1 * np.random.standard_normal((D, 1))), "theta0": f32(np.random.uniform(-1.5, 1.5, (K, P))), "theta1": f32(np.random.uniform(-1.5, 1.5, (K, P))), "offs": striped(np.random.permutation(np.tile(np.arange(S), 2))[:N])}


def reference(table, w, b, theta0, theta1, offs):
    idx = offs[:16].T.reshape(-1)
    u = f64(w).T @ f64(table)[:, idx] + f64(b)
    u0, u1, u2 = u[:, :P], u[:, P:P + P], u[:, P + P:]
    h1 = u0 + rot(f64(theta0), u1)
    h2 = u0 + rot(f64(theta0), u1 + rot(f64(theta1), u2))
    return np.concatenate([u0, h1 / 2.0, h2 / 3.0], axis=1)

@@ -1,0 +1,106 @@
+import math
+
+import concourse.mybir as mybir
+
+FLOPS = 2 * 128 * 128 * 1536
+
+F32 = mybir.dt.float32
+BF16 = mybir.dt.bfloat16
+U16 = mybir.dt.uint16
+ADD = mybir.AluOpType.add
+MULT = mybir.AluOpType.mult
+MAX = mybir.AluOpType.max
+SIN = mybir.ActivationFunctionType.Sin
+IDENTITY = mybir.ActivationFunctionType.Identity
+
+D = 128
+K = 64
+S = 2048
+P = 512
+COLS = P // 16
+
+
+def tile_metapathaggrnet_kernel(tc, table, w, b, theta0, theta1, offs, out):
+    nc = tc.nc
+    with tc.tile_pool(name="held", bufs=1) as held, tc.psum_pool(name="banks", bufs=1) as banks:
+        offsets = held.tile([D, 3 * COLS], U16, name="offsets")
+        nc.sync.dma_start(offsets[:], offs)
+        table_sb = held.tile([D, S], BF16, name="table_sb")
+        nc.sync.dma_start(table_sb[:], table)
+
+        angle0 = held.tile([D, P], F32, name="angle0")
+        angle1 = held.tile([D, P], F32, name="angle1")
+        nc.scalar.dma_start(angle0[0:K, :], theta0)
+        nc.scalar.dma_start(angle0[K:D, :], theta0)
+        nc.scalar.dma_start(angle1[0:K, :], theta1)
+        nc.scalar.dma_start(angle1[K:D, :], theta1)
+
+        w_plain = held.tile([D, D], BF16, name="w_plain")
+        w_swap = held.tile([D, D], BF16, name="w_swap")
+        nc.gpsimd.dma_start(w_plain[:], w)
+        nc.gpsimd.dma_start(w_swap[:, 0:K], w[:, K:D])
+        nc.gpsimd.dma_start(w_swap[:, K:D], w[:, 0:K])
+        b_plain = held.tile([D, 1], F32, name="b_plain")
+        b_swap = held.tile([D, 1], F32, name="b_swap")
+        nc.gpsimd.dma_start(b_plain[:], b)
+        nc.gpsimd.dma_start(b_swap[0:K, :], b[K:D, :])
+        nc.gpsimd.dma_start(b_swap[K:D, :], b[0:K, :])
+
+        sign = held.tile([D, 1], F32, name="sign")
+        nc.vector.memset(sign[0:K, :], -1.0)
+        nc.vector.memset(sign[K:D, :], 1.0)
+        half_pi = held.tile([D, 1], F32, name="half_pi")
+        nc.vector.memset(half_pi[:], math.pi / 2)
+
+        sin0 = held.tile([D, P], F32, name="sin0")
+        cos0 = held.tile([D, P], F32, name="cos0")
+        nc.scalar.activation(sin0[:], angle0[:], SIN, scale=sign[:, 0:1])
+        nc.scalar.activation(cos0[:], angle0[:], SIN, bias=half_pi[:, 0:1])
+
+        angle01 = held.tile([D, P], F32, name="angle01")
+        nc.vector.tensor_tensor(angle01[:], angle0[:], angle1[:], ADD)
+        abs01 = held.tile([D, P], F32, name="abs01")
+        nc.vector.scalar_tensor_tensor(abs01[:], angle01[:], -1.0, angle01[:], MULT, MAX)
+        sin01 = held.tile([D, P], F32, name="sin01")
+        cos01 = held.tile([D, P], F32, name="cos01")
+        nc.scalar.activation(sin01[:], angle01[:], SIN, scale=sign[:, 0:1])
+        nc.scalar.activation(cos01[:], abs01[:], SIN, scale=-1.0, bias=half_pi[:, 0:1])
+
+        def project(weights, node, name):
+            bank = banks.tile([D, P], F32, name=name)
+            picked = table_sb[:].indirect(offsets[:, node * COLS : (node + 1) * COLS])
+            nc.tensor.matmul(bank[:], weights[:], picked, start=True, stop=True)
+            return bank
+
+        p1 = project(w_plain, 1, "p1")
+        p1_swap = project(w_swap, 1, "p1_swap")
+        p0 = project(w_plain, 0, "p0")
+        p2 = project(w_plain, 2, "p2")
+        p2_swap = project(w_swap, 2, "p2_swap")
+
+        def rotate(bank, bank_swap, cos, sin, name):
+            by_cos = held.tile([D, P], F32, name=name + "_cos")
+            by_sin = held.tile([D, P], F32, name=name + "_sin")
+            turned = held.tile([D, P], F32, name=name)
+            nc.vector.scalar_tensor_tensor(by_cos[:], bank[:], b_plain[:, 0:1], cos[:], ADD, MULT)
+            nc.vector.scalar_tensor_tensor(by_sin[:], bank_swap[:], b_swap[:, 0:1], sin[:], ADD, MULT)
+            nc.vector.tensor_tensor(turned[:], by_cos[:], by_sin[:], ADD)
+            return turned
+
+        out0 = held.tile([D, P], F32, name="out0")
+        nc.scalar.activation(out0[:], p0[:], IDENTITY, bias=b_plain[:, 0:1])
+        nc.sync.dma_start(out[:, 0:P], out0[:])
+
+        turned1 = rotate(p1, p1_swap, cos0, sin0, "turned1")
+        h1 = held.tile([D, P], F32, name="h1")
+        nc.vector.tensor_tensor(h1[:], turned1[:], out0[:], ADD)
+        out1 = held.tile([D, P], F32, name="out1")
+        nc.scalar.mul(out1[:], h1[:], 1.0 / 2.0)
+        nc.sync.dma_start(out[:, P : 2 * P], out1[:])
+
+        turned2 = rotate(p2, p2_swap, cos01, sin01, "turned2")
+        h2 = held.tile([D, P], F32, name="h2")
+        nc.vector.tensor_tensor(h2[:], turned2[:], h1[:], ADD)
+        out2 = held.tile([D, P], F32, name="out2")
+        nc.scalar.mul(out2[:], h2[:], 1.0 / 3.0)
+        nc.sync.dma_start(out[:, 2 * P : 3 * P], out2[:])

@@ -24,38 +24,37 @@ def tile_metapathaggrnet_kernel(tc, table, w, b, theta0, theta1, offs, out):
     nc = tc.nc
     with tc.tile_pool(name="held", bufs=1) as held, tc.psum_pool(name="banks", bufs=1) as banks:
         offsets = held.tile([D, 3 * COLS], U16, name="offsets")
-        nc.sync.dma_start(offsets[:], offs)
         table_sb = held.tile([D, S], BF16, name="table_sb")
-        nc.sync.dma_start(table_sb[:], table)
-
         angle0 = held.tile([D, P], F32, name="angle0")
         angle1 = held.tile([D, P], F32, name="angle1")
-        nc.scalar.dma_start(angle0[0:K, :], theta0)
-        nc.scalar.dma_start(angle0[K:D, :], theta0)
-        nc.scalar.dma_start(angle1[0:K, :], theta1)
-        nc.scalar.dma_start(angle1[K:D, :], theta1)
+        w_twice = held.tile([D, D + K], BF16, name="w_twice")
+        b_twice = held.tile([1, D + K], F32, name="b_twice")
 
-        w_plain = held.tile([D, D], BF16, name="w_plain")
-        w_swap = held.tile([D, D], BF16, name="w_swap")
-        nc.gpsimd.dma_start(w_plain[:], w)
-        nc.gpsimd.dma_start(w_swap[:, 0:K], w[:, K:D])
-        nc.gpsimd.dma_start(w_swap[:, K:D], w[:, 0:K])
-        b_plain = held.tile([D, 1], F32, name="b_plain")
-        b_swap = held.tile([D, 1], F32, name="b_swap")
-        nc.gpsimd.dma_start(b_plain[:], b)
-        nc.gpsimd.dma_start(b_swap[0:K, :], b[K:D, :])
-        nc.gpsimd.dma_start(b_swap[K:D, :], b[0:K, :])
+        nc.scalar.dma_start(b_twice[0:1, 0:D], b.rearrange("d o -> o d"))
+        nc.gpsimd.dma_start(w_twice[:, 0:D], w)
+        nc.sync.dma_start(angle0[0:K, :], theta0)
+        nc.scalar.dma_start(angle0[K:D, :], theta0)
+        nc.sync.dma_start(angle1[0:K, :], theta1)
+        nc.scalar.dma_start(angle1[K:D, :], theta1)
+        nc.sync.dma_start(offsets[:], offs)
+        nc.sync.dma_start(table_sb[:, 0 : S // 2], table[:, 0 : S // 2])
+        nc.scalar.dma_start(table_sb[:, S // 2 : S], table[:, S // 2 : S])
+
+        nc.gpsimd.tensor_copy(w_twice[:, D : D + K], w_twice[:, 0:K])
+        nc.gpsimd.tensor_copy(b_twice[0:1, D : D + K], b_twice[0:1, 0:K])
 
         sign = held.tile([D, 1], F32, name="sign")
         nc.vector.memset(sign[0:K, :], -1.0)
         nc.vector.memset(sign[K:D, :], 1.0)
         half_pi = held.tile([D, 1], F32, name="half_pi")
         nc.vector.memset(half_pi[:], math.pi / 2)
+        first_sin = held.tile([D, 1], F32, name="first_sin")
+        nc.scalar.activation(first_sin[:], half_pi[:], SIN)
 
         sin0 = held.tile([D, P], F32, name="sin0")
         cos0 = held.tile([D, P], F32, name="cos0")
-        nc.scalar.activation(sin0[:], angle0[:], SIN, scale=sign[:, 0:1])
         nc.scalar.activation(cos0[:], angle0[:], SIN, bias=half_pi[:, 0:1])
+        nc.scalar.activation(sin0[:], angle0[:], SIN, scale=sign[:, 0:1])
 
         angle01 = held.tile([D, P], F32, name="angle01")
         nc.vector.tensor_tensor(angle01[:], angle0[:], angle1[:], ADD)
@@ -65,11 +64,28 @@ def tile_metapathaggrnet_kernel(tc, table, w, b, theta0, theta1, offs, out):
         cos01 = held.tile([D, P], F32, name="cos01")
         nc.scalar.activation(sin01[:], angle01[:], SIN, scale=sign[:, 0:1])
         nc.scalar.activation(cos01[:], abs01[:], SIN, scale=-1.0, bias=half_pi[:, 0:1])
+        cos01_third = held.tile([D, P], F32, name="cos01_third")
+        sin01_third = held.tile([D, P], F32, name="sin01_third")
+        nc.scalar.mul(cos01_third[:], cos01[:], 1.0 / 3.0)
+        nc.scalar.mul(sin01_third[:], sin01[:], 1.0 / 3.0)
+
+        one = held.tile([1, 1], F32, name="one")
+        nc.vector.memset(one[:], 1.0)
+        bias_bank = banks.tile([D, 2], F32, name="bias_bank")
+        nc.tensor.matmul(bias_bank[:, 0:1], b_twice[0:1, 0:D], one[:], start=True, stop=True)
+        nc.tensor.matmul(bias_bank[:, 1:2], b_twice[0:1, K : K + D], one[:], start=True, stop=True)
+        bias = held.tile([D, 2], F32, name="bias")
+        nc.vector.tensor_copy(bias[:], bias_bank[:])
+        b_plain = bias[:, 0:1]
+        b_swap = bias[:, 1:2]
+
+        w_plain = w_twice[:, 0:D]
+        w_swap = w_twice[:, K : K + D]
 
         def project(weights, node, name):
             bank = banks.tile([D, P], F32, name=name)
             picked = table_sb[:].indirect(offsets[:, node * COLS : (node + 1) * COLS])
-            nc.tensor.matmul(bank[:], weights[:], picked, start=True, stop=True)
+            nc.tensor.matmul(bank[:], weights, picked, start=True, stop=True)
             return bank
 
         p1 = project(w_plain, 1, "p1")
@@ -78,29 +94,30 @@ def tile_metapathaggrnet_kernel(tc, table, w, b, theta0, theta1, offs, out):
         p2 = project(w_plain, 2, "p2")
         p2_swap = project(w_swap, 2, "p2_swap")
 
-        def rotate(bank, bank_swap, cos, sin, name):
-            by_cos = held.tile([D, P], F32, name=name + "_cos")
-            by_sin = held.tile([D, P], F32, name=name + "_sin")
-            turned = held.tile([D, P], F32, name=name)
-            nc.vector.scalar_tensor_tensor(by_cos[:], bank[:], b_plain[:, 0:1], cos[:], ADD, MULT)
-            nc.vector.scalar_tensor_tensor(by_sin[:], bank_swap[:], b_swap[:, 0:1], sin[:], ADD, MULT)
-            nc.vector.tensor_tensor(turned[:], by_cos[:], by_sin[:], ADD)
-            return turned
+        def work(name):
+            return held.tile([D, P], F32, name=name)
 
-        out0 = held.tile([D, P], F32, name="out0")
-        nc.scalar.activation(out0[:], p0[:], IDENTITY, bias=b_plain[:, 0:1])
+        u1_cos = work("u1_cos")
+        nc.vector.scalar_tensor_tensor(u1_cos[:], p1[:], b_plain, cos0[:], ADD, MULT)
+        u1_sin = work("u1_sin")
+        nc.vector.scalar_tensor_tensor(u1_sin[:], p1_swap[:], b_swap, sin0[:], ADD, MULT)
+        u0_u1_cos = work("u0_u1_cos")
+        nc.vector.scalar_tensor_tensor(u0_u1_cos[:], p0[:], b_plain, u1_cos[:], ADD, ADD)
+        u2_cos = work("u2_cos")
+        nc.vector.scalar_tensor_tensor(u2_cos[:], p2[:], b_plain, cos01_third[:], ADD, MULT)
+        h1 = work("h1")
+        nc.vector.tensor_tensor(h1[:], u0_u1_cos[:], u1_sin[:], ADD)
+        u2_sin = work("u2_sin")
+        nc.vector.scalar_tensor_tensor(u2_sin[:], p2_swap[:], b_swap, sin01_third[:], ADD, MULT)
+        h1_u2_cos = work("h1_u2_cos")
+        nc.vector.scalar_tensor_tensor(h1_u2_cos[:], h1[:], 1.0 / 3.0, u2_cos[:], MULT, ADD)
+        out2 = work("out2")
+        nc.vector.tensor_tensor(out2[:], h1_u2_cos[:], u2_sin[:], ADD)
+        nc.sync.dma_start(out[:, 2 * P : 3 * P], out2[:])
+
+        out0 = work("out0")
+        nc.scalar.activation(out0[:], p0[:], IDENTITY, bias=b_plain)
         nc.sync.dma_start(out[:, 0:P], out0[:])
-
-        turned1 = rotate(p1, p1_swap, cos0, sin0, "turned1")
-        h1 = held.tile([D, P], F32, name="h1")
-        nc.vector.tensor_tensor(h1[:], turned1[:], out0[:], ADD)
-        out1 = held.tile([D, P], F32, name="out1")
+        out1 = work("out1")
         nc.scalar.mul(out1[:], h1[:], 1.0 / 2.0)
         nc.sync.dma_start(out[:, P : 2 * P], out1[:])
-
-        turned2 = rotate(p2, p2_swap, cos01, sin01, "turned2")
-        h2 = held.tile([D, P], F32, name="h2")
-        nc.vector.tensor_tensor(h2[:], turned2[:], h1[:], ADD)
-        out2 = held.tile([D, P], F32, name="out2")
-        nc.scalar.mul(out2[:], h2[:], 1.0 / 3.0)
-        nc.sync.dma_start(out[:, 2 * P : 3 * P], out2[:])

@@ -18,6 +18,7 @@ K = 64
 S = 2048
 P = 512
 COLS = P // 16
+WARM_UP_MATMULS = 12
 
 
 def tile_metapathaggrnet_kernel(tc, table, w, b, theta0, theta1, offs, out):
@@ -28,9 +29,9 @@ def tile_metapathaggrnet_kernel(tc, table, w, b, theta0, theta1, offs, out):
         angle0 = held.tile([D, P], F32, name="angle0")
         angle1 = held.tile([D, P], F32, name="angle1")
         w_twice = held.tile([D, D + K], BF16, name="w_twice")
-        b_twice = held.tile([1, D + K], F32, name="b_twice")
+        b_plain = held.tile([D, 1], F32, name="b_plain")
+        b_swap = held.tile([D, 1], F32, name="b_swap")
 
-        nc.scalar.dma_start(b_twice[0:1, 0:D], b.rearrange("d o -> o d"))
         nc.gpsimd.dma_start(w_twice[:, 0:D], w)
         nc.sync.dma_start(angle0[0:K, :], theta0)
         nc.scalar.dma_start(angle0[K:D, :], theta0)
@@ -39,9 +40,17 @@ def tile_metapathaggrnet_kernel(tc, table, w, b, theta0, theta1, offs, out):
         nc.sync.dma_start(offsets[:], offs)
         nc.sync.dma_start(table_sb[:, 0 : S // 2], table[:, 0 : S // 2])
         nc.scalar.dma_start(table_sb[:, S // 2 : S], table[:, S // 2 : S])
+        nc.sync.dma_start(b_plain[:], b)
+        nc.scalar.dma_start(b_swap[0:K, :], b[K:D, :])
+        nc.scalar.dma_start(b_swap[K:D, :], b[0:K, :])
 
         nc.gpsimd.tensor_copy(w_twice[:, D : D + K], w_twice[:, 0:K])
-        nc.gpsimd.tensor_copy(b_twice[0:1, D : D + K], b_twice[0:1, 0:K])
+
+        zeros = held.tile([D, P], BF16, name="zeros")
+        nc.vector.memset(zeros[:], 0.0)
+        idle_bank = banks.tile([D, P], F32, name="idle_bank")
+        for step in range(WARM_UP_MATMULS):
+            nc.tensor.matmul(idle_bank[:], zeros[:, 0:D], zeros[:], start=True, stop=True)
 
         sign = held.tile([D, 1], F32, name="sign")
         nc.vector.memset(sign[0:K, :], -1.0)
@@ -69,16 +78,6 @@ def tile_metapathaggrnet_kernel(tc, table, w, b, theta0, theta1, offs, out):
         nc.scalar.mul(cos01_third[:], cos01[:], 1.0 / 3.0)
         nc.scalar.mul(sin01_third[:], sin01[:], 1.0 / 3.0)
 
-        one = held.tile([1, 1], F32, name="one")
-        nc.vector.memset(one[:], 1.0)
-        bias_bank = banks.tile([D, 2], F32, name="bias_bank")
-        nc.tensor.matmul(bias_bank[:, 0:1], b_twice[0:1, 0:D], one[:], start=True, stop=True)
-        nc.tensor.matmul(bias_bank[:, 1:2], b_twice[0:1, K : K + D], one[:], start=True, stop=True)
-        bias = held.tile([D, 2], F32, name="bias")
-        nc.vector.tensor_copy(bias[:], bias_bank[:])
-        b_plain = bias[:, 0:1]
-        b_swap = bias[:, 1:2]
-
         w_plain = w_twice[:, 0:D]
         w_swap = w_twice[:, K : K + D]
 
@@ -98,17 +97,17 @@ def tile_metapathaggrnet_kernel(tc, table, w, b, theta0, theta1, offs, out):
             return held.tile([D, P], F32, name=name)
 
         u1_cos = work("u1_cos")
-        nc.vector.scalar_tensor_tensor(u1_cos[:], p1[:], b_plain, cos0[:], ADD, MULT)
+        nc.vector.scalar_tensor_tensor(u1_cos[:], p1[:], b_plain[:, 0:1], cos0[:], ADD, MULT)
         u1_sin = work("u1_sin")
-        nc.vector.scalar_tensor_tensor(u1_sin[:], p1_swap[:], b_swap, sin0[:], ADD, MULT)
+        nc.vector.scalar_tensor_tensor(u1_sin[:], p1_swap[:], b_swap[:, 0:1], sin0[:], ADD, MULT)
         u0_u1_cos = work("u0_u1_cos")
-        nc.vector.scalar_tensor_tensor(u0_u1_cos[:], p0[:], b_plain, u1_cos[:], ADD, ADD)
+        nc.vector.scalar_tensor_tensor(u0_u1_cos[:], p0[:], b_plain[:, 0:1], u1_cos[:], ADD, ADD)
         u2_cos = work("u2_cos")
-        nc.vector.scalar_tensor_tensor(u2_cos[:], p2[:], b_plain, cos01_third[:], ADD, MULT)
+        nc.vector.scalar_tensor_tensor(u2_cos[:], p2[:], b_plain[:, 0:1], cos01_third[:], ADD, MULT)
         h1 = work("h1")
         nc.vector.tensor_tensor(h1[:], u0_u1_cos[:], u1_sin[:], ADD)
         u2_sin = work("u2_sin")
-        nc.vector.scalar_tensor_tensor(u2_sin[:], p2_swap[:], b_swap, sin01_third[:], ADD, MULT)
+        nc.vector.scalar_tensor_tensor(u2_sin[:], p2_swap[:], b_swap[:, 0:1], sin01_third[:], ADD, MULT)
         h1_u2_cos = work("h1_u2_cos")
         nc.vector.scalar_tensor_tensor(h1_u2_cos[:], h1[:], 1.0 / 3.0, u2_cos[:], MULT, ADD)
         out2 = work("out2")
@@ -116,7 +115,7 @@ def tile_metapathaggrnet_kernel(tc, table, w, b, theta0, theta1, offs, out):
         nc.sync.dma_start(out[:, 2 * P : 3 * P], out2[:])
 
         out0 = work("out0")
-        nc.scalar.activation(out0[:], p0[:], IDENTITY, bias=b_plain)
+        nc.scalar.activation(out0[:], p0[:], IDENTITY, bias=b_plain[:, 0:1])
         nc.sync.dma_start(out[:, 0:P], out0[:])
         out1 = work("out1")
         nc.scalar.mul(out1[:], h1[:], 1.0 / 2.0)

@@ -96,26 +96,39 @@ def tile_metapathaggrnet_kernel(tc, table, w, b, theta0, theta1, offs, out):
         def work(name):
             return held.tile([D, P], F32, name=name)
 
+        halves = [slice(first, first + P // 2) for first in (0, P // 2)]
+        out2_halves = [slice(2 * P + first, 2 * P + first + P // 2) for first in (0, P // 2)]
+        b_u = b_plain[:, 0:1]
+        b_swap_u = b_swap[:, 0:1]
+
         u1_cos = work("u1_cos")
-        nc.vector.scalar_tensor_tensor(u1_cos[:], p1[:], b_plain[:, 0:1], cos0[:], ADD, MULT)
+        for cols in halves:
+            nc.vector.scalar_tensor_tensor(u1_cos[:, cols], p1[:, cols], b_u, cos0[:, cols], ADD, MULT)
         u1_sin = work("u1_sin")
-        nc.vector.scalar_tensor_tensor(u1_sin[:], p1_swap[:], b_swap[:, 0:1], sin0[:], ADD, MULT)
+        for cols in halves:
+            nc.vector.scalar_tensor_tensor(u1_sin[:, cols], p1_swap[:, cols], b_swap_u, sin0[:, cols], ADD, MULT)
         u0_u1_cos = work("u0_u1_cos")
-        nc.vector.scalar_tensor_tensor(u0_u1_cos[:], p0[:], b_plain[:, 0:1], u1_cos[:], ADD, ADD)
+        for cols in halves:
+            nc.vector.scalar_tensor_tensor(u0_u1_cos[:, cols], p0[:, cols], b_u, u1_cos[:, cols], ADD, ADD)
         u2_cos = work("u2_cos")
-        nc.vector.scalar_tensor_tensor(u2_cos[:], p2[:], b_plain[:, 0:1], cos01_third[:], ADD, MULT)
+        for cols in halves:
+            nc.vector.scalar_tensor_tensor(u2_cos[:, cols], p2[:, cols], b_u, cos01_third[:, cols], ADD, MULT)
         h1 = work("h1")
-        nc.vector.tensor_tensor(h1[:], u0_u1_cos[:], u1_sin[:], ADD)
+        for cols in halves:
+            nc.vector.tensor_tensor(h1[:, cols], u0_u1_cos[:, cols], u1_sin[:, cols], ADD)
         u2_sin = work("u2_sin")
-        nc.vector.scalar_tensor_tensor(u2_sin[:], p2_swap[:], b_swap[:, 0:1], sin01_third[:], ADD, MULT)
+        for cols in halves:
+            nc.vector.scalar_tensor_tensor(u2_sin[:, cols], p2_swap[:, cols], b_swap_u, sin01_third[:, cols], ADD, MULT)
         h1_u2_cos = work("h1_u2_cos")
-        nc.vector.scalar_tensor_tensor(h1_u2_cos[:], h1[:], 1.0 / 3.0, u2_cos[:], MULT, ADD)
+        for cols in halves:
+            nc.vector.scalar_tensor_tensor(h1_u2_cos[:, cols], h1[:, cols], 1.0 / 3.0, u2_cos[:, cols], MULT, ADD)
         out2 = work("out2")
-        nc.vector.tensor_tensor(out2[:], h1_u2_cos[:], u2_sin[:], ADD)
-        nc.sync.dma_start(out[:, 2 * P : 3 * P], out2[:])
+        for cols, out_cols, queue in zip(halves, out2_halves, (nc.sync, nc.scalar)):
+            nc.vector.tensor_tensor(out2[:, cols], h1_u2_cos[:, cols], u2_sin[:, cols], ADD)
+            queue.dma_start(out[:, out_cols], out2[:, cols])
 
         out0 = work("out0")
-        nc.scalar.activation(out0[:], p0[:], IDENTITY, bias=b_plain[:, 0:1])
+        nc.scalar.activation(out0[:], p0[:], IDENTITY, bias=b_u)
         nc.sync.dma_start(out[:, 0:P], out0[:])
         out1 = work("out1")
         nc.scalar.mul(out1[:], h1[:], 1.0 / 2.0)

@@ -18,7 +18,7 @@ K = 64
 S = 2048
 P = 512
 COLS = P // 16
-WARM_UP_MATMULS = 12
+WARM_UP_MATMULS = 8
 
 
 def tile_metapathaggrnet_kernel(tc, table, w, b, theta0, theta1, offs, out):

@@ -81,17 +81,17 @@ def tile_metapathaggrnet_kernel(tc, table, w, b, theta0, theta1, offs, out):
         w_plain = w_twice[:, 0:D]
         w_swap = w_twice[:, K : K + D]
 
-        def project(weights, node, name):
-            bank = banks.tile([D, P], F32, name=name)
-            picked = table_sb[:].indirect(offsets[:, node * COLS : (node + 1) * COLS])
+        def project(weights, first_col, cols, name):
+            bank = banks.tile([D, 16 * cols], F32, name=name)
+            picked = table_sb[:].indirect(offsets[:, first_col : first_col + cols])
             nc.tensor.matmul(bank[:], weights, picked, start=True, stop=True)
             return bank
 
-        p1 = project(w_plain, 1, "p1")
-        p1_swap = project(w_swap, 1, "p1_swap")
-        p0 = project(w_plain, 0, "p0")
-        p2 = project(w_plain, 2, "p2")
-        p2_swap = project(w_swap, 2, "p2_swap")
+        p1 = [project(w_plain, COLS + half * COLS // 2, COLS // 2, "p1_%d" % half) for half in (0, 1)]
+        p1_swap = [project(w_swap, COLS + half * COLS // 2, COLS // 2, "p1_swap_%d" % half) for half in (0, 1)]
+        p0 = project(w_plain, 0, COLS, "p0")
+        p2 = project(w_plain, 2 * COLS, COLS, "p2")
+        p2_swap = project(w_swap, 2 * COLS, COLS, "p2_swap")
 
         def work(name):
             return held.tile([D, P], F32, name=name)
@@ -102,20 +102,20 @@ def tile_metapathaggrnet_kernel(tc, table, w, b, theta0, theta1, offs, out):
         b_swap_u = b_swap[:, 0:1]
 
         u1_cos = work("u1_cos")
-        for cols in halves:
-            nc.vector.scalar_tensor_tensor(u1_cos[:, cols], p1[:, cols], b_u, cos0[:, cols], ADD, MULT)
+        for half, cols in enumerate(halves):
+            nc.vector.scalar_tensor_tensor(u1_cos[:, cols], p1[half][:], b_u, cos0[:, cols], ADD, MULT)
         u1_sin = work("u1_sin")
+        for half, cols in enumerate(halves):
+            nc.vector.scalar_tensor_tensor(u1_sin[:, cols], p1_swap[half][:], b_swap_u, sin0[:, cols], ADD, MULT)
+        u1_turned = work("u1_turned")
         for cols in halves:
-            nc.vector.scalar_tensor_tensor(u1_sin[:, cols], p1_swap[:, cols], b_swap_u, sin0[:, cols], ADD, MULT)
-        u0_u1_cos = work("u0_u1_cos")
+            nc.vector.tensor_tensor(u1_turned[:, cols], u1_cos[:, cols], u1_sin[:, cols], ADD)
+        h1 = work("h1")
         for cols in halves:
-            nc.vector.scalar_tensor_tensor(u0_u1_cos[:, cols], p0[:, cols], b_u, u1_cos[:, cols], ADD, ADD)
+            nc.vector.scalar_tensor_tensor(h1[:, cols], p0[:, cols], b_u, u1_turned[:, cols], ADD, ADD)
         u2_cos = work("u2_cos")
         for cols in halves:
             nc.vector.scalar_tensor_tensor(u2_cos[:, cols], p2[:, cols], b_u, cos01_third[:, cols], ADD, MULT)
-        h1 = work("h1")
-        for cols in halves:
-            nc.vector.tensor_tensor(h1[:, cols], u0_u1_cos[:, cols], u1_sin[:, cols], ADD)
         u2_sin = work("u2_sin")
         for cols in halves:
             nc.vector.scalar_tensor_tensor(u2_sin[:, cols], p2_swap[:, cols], b_swap_u, sin01_third[:, cols], ADD, MULT)

@@ -8,6 +8,7 @@ F32 = mybir.dt.float32
 BF16 = mybir.dt.bfloat16
 U16 = mybir.dt.uint16
 ADD = mybir.AluOpType.add
+SUBTRACT = mybir.AluOpType.subtract
 MULT = mybir.AluOpType.mult
 MAX = mybir.AluOpType.max
 SIN = mybir.ActivationFunctionType.Sin
@@ -17,119 +18,122 @@ D = 128
 K = 64
 S = 2048
 P = 512
-COLS = P // 16
-WARM_UP_MATMULS = 8
+HALF = P // 2
+COLS = HALF // 16
+RE, IM = 0, 1
+WARM_UP_MATMULS = 4
 
 
 def tile_metapathaggrnet_kernel(tc, table, w, b, theta0, theta1, offs, out):
     nc = tc.nc
     with tc.tile_pool(name="held", bufs=1) as held, tc.psum_pool(name="banks", bufs=1) as banks:
-        offsets = held.tile([D, 3 * COLS], U16, name="offsets")
-        table_sb = held.tile([D, S], BF16, name="table_sb")
-        angle0 = held.tile([D, P], F32, name="angle0")
-        angle1 = held.tile([D, P], F32, name="angle1")
-        w_twice = held.tile([D, D + K], BF16, name="w_twice")
-        b_plain = held.tile([D, 1], F32, name="b_plain")
-        b_swap = held.tile([D, 1], F32, name="b_swap")
 
-        nc.gpsimd.dma_start(w_twice[:, 0:D], w)
-        nc.sync.dma_start(angle0[0:K, :], theta0)
-        nc.scalar.dma_start(angle0[K:D, :], theta0)
-        nc.sync.dma_start(angle1[0:K, :], theta1)
-        nc.scalar.dma_start(angle1[K:D, :], theta1)
-        nc.sync.dma_start(offsets[:], offs)
-        nc.sync.dma_start(table_sb[:, 0 : S // 2], table[:, 0 : S // 2])
-        nc.scalar.dma_start(table_sb[:, S // 2 : S], table[:, S // 2 : S])
-        nc.sync.dma_start(b_plain[:], b)
-        nc.scalar.dma_start(b_swap[0:K, :], b[K:D, :])
-        nc.scalar.dma_start(b_swap[K:D, :], b[0:K, :])
+        def f32_tile(name, cols=HALF):
+            return held.tile([D, cols], F32, name=name)
 
-        nc.gpsimd.tensor_copy(w_twice[:, D : D + K], w_twice[:, 0:K])
-
+        half_pi = f32_tile("half_pi", 1)
+        nc.vector.memset(half_pi[:], math.pi / 2)
         zeros = held.tile([D, P], BF16, name="zeros")
         nc.vector.memset(zeros[:], 0.0)
+        b_raw = held.tile([D, 2, 16], F32, name="b_raw")
+        nc.gpsimd.memset(b_raw[:], 0.0)
+        w_spread = held.tile([D, 2, 2, K, 2], BF16, name="w_spread")
+        nc.gpsimd.memset(w_spread[:], 0.0)
+
+        w_sb = held.tile([D, D], BF16, name="w_sb")
+        nc.sync.dma_start(w_sb[:], w)
+        offsets = held.tile([D, 6 * COLS], U16, name="offsets")
+        nc.sync.dma_start(offsets[:], offs)
+        nc.sync.dma_start(b_raw[::32], b.rearrange("(r g i) o -> g r (i o)", r=2, g=4))
+        table_sb = held.tile([D, S], BF16, name="table_sb")
+        nc.sync.dma_start(table_sb[:], table)
+        first_sin = f32_tile("first_sin", 1)
+        nc.scalar.activation(first_sin[:], half_pi[:], SIN)
+        angle0 = f32_tile("angle0")
+        nc.scalar.dma_start(angle0[:], theta0.rearrange("k (h p) -> (k h) p", h=2))
+        angle1 = f32_tile("angle1")
+        nc.scalar.dma_start(angle1[:], theta1.rearrange("k (h p) -> (k h) p", h=2))
+
+        b_twice = held.tile([D, 2, 16, 2], F32, name="b_twice", align_bytes=64)
+        nc.vector.tensor_copy(b_twice[:], b_raw[:].unsqueeze(3).to_broadcast([D, 2, 16, 2]))
+        bias_sb = held.tile([D, 2, 32], F32, name="bias_sb", align_bytes=64)
+        for part in (RE, IM):
+            nc.vector.transpose(bias_sb[:, part, :], b_twice[:, part].rearrange("q i j -> q (i j)"))
+        bias = [bias_sb[:, part, 0:1] for part in (RE, IM)]
+
         idle_bank = banks.tile([D, P], F32, name="idle_bank")
         for step in range(WARM_UP_MATMULS):
             nc.tensor.matmul(idle_bank[:], zeros[:, 0:D], zeros[:], start=True, stop=True)
 
-        sign = held.tile([D, 1], F32, name="sign")
-        nc.vector.memset(sign[0:K, :], -1.0)
-        nc.vector.memset(sign[K:D, :], 1.0)
-        half_pi = held.tile([D, 1], F32, name="half_pi")
-        nc.vector.memset(half_pi[:], math.pi / 2)
-        first_sin = held.tile([D, 1], F32, name="first_sin")
-        nc.scalar.activation(first_sin[:], half_pi[:], SIN)
-
-        sin0 = held.tile([D, P], F32, name="sin0")
-        cos0 = held.tile([D, P], F32, name="cos0")
+        for half in (0, 1):
+            nc.scalar.copy(w_spread[:, :, half, :, half], w_sb[:].rearrange("d (r k) -> d r k", r=2))
+        cos0 = f32_tile("cos0")
         nc.scalar.activation(cos0[:], angle0[:], SIN, bias=half_pi[:, 0:1])
-        nc.scalar.activation(sin0[:], angle0[:], SIN, scale=sign[:, 0:1])
-
-        angle01 = held.tile([D, P], F32, name="angle01")
+        sin0 = f32_tile("sin0")
+        nc.scalar.activation(sin0[:], angle0[:], SIN)
+        angle01 = f32_tile("angle01")
         nc.vector.tensor_tensor(angle01[:], angle0[:], angle1[:], ADD)
-        abs01 = held.tile([D, P], F32, name="abs01")
+        abs01 = f32_tile("abs01")
         nc.vector.scalar_tensor_tensor(abs01[:], angle01[:], -1.0, angle01[:], MULT, MAX)
-        sin01 = held.tile([D, P], F32, name="sin01")
-        cos01 = held.tile([D, P], F32, name="cos01")
-        nc.scalar.activation(sin01[:], angle01[:], SIN, scale=sign[:, 0:1])
+        cos01 = f32_tile("cos01")
+        sin01 = f32_tile("sin01")
+        nc.scalar.activation(sin01[:], angle01[:], SIN)
         nc.scalar.activation(cos01[:], abs01[:], SIN, scale=-1.0, bias=half_pi[:, 0:1])
-        cos01_third = held.tile([D, P], F32, name="cos01_third")
-        sin01_third = held.tile([D, P], F32, name="sin01_third")
+        cos01_third = f32_tile("cos01_third")
+        sin01_third = f32_tile("sin01_third")
         nc.scalar.mul(cos01_third[:], cos01[:], 1.0 / 3.0)
         nc.scalar.mul(sin01_third[:], sin01[:], 1.0 / 3.0)
 
-        w_plain = w_twice[:, 0:D]
-        w_swap = w_twice[:, K : K + D]
-
-        def project(weights, first_col, cols, name):
-            bank = banks.tile([D, 16 * cols], F32, name=name)
-            picked = table_sb[:].indirect(offsets[:, first_col : first_col + cols])
-            nc.tensor.matmul(bank[:], weights, picked, start=True, stop=True)
+        def project(node, part):
+            bank = banks.tile([D, HALF], F32, name="node%d_part%d" % (node, part))
+            for half in (0, 1):
+                first = (2 * node + half) * COLS
+                picked = table_sb[:].indirect(offsets[:, first : first + COLS])
+                weights = w_spread[:, part, half].rearrange("d k j -> d (k j)")
+                nc.tensor.matmul(bank[:], weights, picked, start=(half == 0), stop=(half == 1))
             return bank
 
-        p1 = [project(w_plain, COLS + half * COLS // 2, COLS // 2, "p1_%d" % half) for half in (0, 1)]
-        p1_swap = [project(w_swap, COLS + half * COLS // 2, COLS // 2, "p1_swap_%d" % half) for half in (0, 1)]
-        p0 = project(w_plain, 0, COLS, "p0")
-        p2 = project(w_plain, 2 * COLS, COLS, "p2")
-        p2_swap = project(w_swap, 2 * COLS, COLS, "p2_swap")
+        node1 = [project(1, part) for part in (RE, IM)]
+        node0 = [project(0, part) for part in (RE, IM)]
+        node2 = [project(2, part) for part in (RE, IM)]
 
-        def work(name):
-            return held.tile([D, P], F32, name=name)
+        def product(name, bank, part, factor):
+            tile = f32_tile(name)
+            nc.vector.scalar_tensor_tensor(tile[:], bank[part][:], bias[part], factor[:], ADD, MULT)
+            return tile
 
-        halves = [slice(first, first + P // 2) for first in (0, P // 2)]
-        out2_halves = [slice(2 * P + first, 2 * P + first + P // 2) for first in (0, P // 2)]
-        b_u = b_plain[:, 0:1]
-        b_swap_u = b_swap[:, 0:1]
+        out0 = held.tile([D, 2, HALF], F32, name="out0")
+        turned1 = held.tile([D, 2, HALF], F32, name="turned1")
+        h1 = held.tile([D, 2, HALF], F32, name="h1")
+        out1 = held.tile([D, 2, HALF], F32, name="out1")
+        partly2 = held.tile([D, 2, HALF], F32, name="partly2")
+        out2 = held.tile([D, 2, HALF], F32, name="out2")
+        stores = out.rearrange("(r k) (s h p) -> s h k r p", r=2, s=3, h=2)
 
-        u1_cos = work("u1_cos")
-        for half, cols in enumerate(halves):
-            nc.vector.scalar_tensor_tensor(u1_cos[:, cols], p1[half][:], b_u, cos0[:, cols], ADD, MULT)
-        u1_sin = work("u1_sin")
-        for half, cols in enumerate(halves):
-            nc.vector.scalar_tensor_tensor(u1_sin[:, cols], p1_swap[half][:], b_swap_u, sin0[:, cols], ADD, MULT)
-        u1_turned = work("u1_turned")
-        for cols in halves:
-            nc.vector.tensor_tensor(u1_turned[:, cols], u1_cos[:, cols], u1_sin[:, cols], ADD)
-        h1 = work("h1")
-        for cols in halves:
-            nc.vector.scalar_tensor_tensor(h1[:, cols], p0[:, cols], b_u, u1_turned[:, cols], ADD, ADD)
-        u2_cos = work("u2_cos")
-        for cols in halves:
-            nc.vector.scalar_tensor_tensor(u2_cos[:, cols], p2[:, cols], b_u, cos01_third[:, cols], ADD, MULT)
-        u2_sin = work("u2_sin")
-        for cols in halves:
-            nc.vector.scalar_tensor_tensor(u2_sin[:, cols], p2_swap[:, cols], b_swap_u, sin01_third[:, cols], ADD, MULT)
-        h1_u2_cos = work("h1_u2_cos")
-        for cols in halves:
-            nc.vector.scalar_tensor_tensor(h1_u2_cos[:, cols], h1[:, cols], 1.0 / 3.0, u2_cos[:, cols], MULT, ADD)
-        out2 = work("out2")
-        for cols, out_cols, queue in zip(halves, out2_halves, (nc.sync, nc.scalar)):
-            nc.vector.tensor_tensor(out2[:, cols], h1_u2_cos[:, cols], u2_sin[:, cols], ADD)
-            queue.dma_start(out[:, out_cols], out2[:, cols])
+        for part in (RE, IM):
+            nc.scalar.activation(out0[:, part, :], node0[part][:], IDENTITY, bias=bias[part])
+        for half in (0, 1):
+            nc.sync.dma_start(stores[0, half], out0[half::2])
 
-        out0 = work("out0")
-        nc.scalar.activation(out0[:], p0[:], IDENTITY, bias=b_u)
-        nc.sync.dma_start(out[:, 0:P], out0[:])
-        out1 = work("out1")
-        nc.scalar.mul(out1[:], h1[:], 1.0 / 2.0)
-        nc.sync.dma_start(out[:, P : 2 * P], out1[:])
+        re_cos1 = product("re_cos1", node1, RE, cos0)
+        re_sin1 = product("re_sin1", node1, RE, sin0)
+        im_sin1 = product("im_sin1", node1, IM, sin0)
+        im_cos1 = product("im_cos1", node1, IM, cos0)
+        nc.vector.tensor_tensor(turned1[:, RE, :], re_cos1[:], im_sin1[:], SUBTRACT)
+        nc.vector.tensor_tensor(turned1[:, IM, :], re_sin1[:], im_cos1[:], ADD)
+        for part in (RE, IM):
+            nc.vector.tensor_tensor(h1[:, part, :], out0[:, part, :], turned1[:, part, :], ADD)
+            nc.scalar.mul(out1[:, part, :], h1[:, part, :], 1.0 / 2.0)
+        for half in (0, 1):
+            nc.sync.dma_start(stores[1, half], out1[half::2])
+
+        re_cos2 = product("re_cos2", node2, RE, cos01_third)
+        re_sin2 = product("re_sin2", node2, RE, sin01_third)
+        for part, made in ((RE, re_cos2), (IM, re_sin2)):
+            nc.vector.scalar_tensor_tensor(partly2[:, part, :], h1[:, part, :], 1.0 / 3.0, made[:], MULT, ADD)
+        im_sin2 = product("im_sin2", node2, IM, sin01_third)
+        im_cos2 = product("im_cos2", node2, IM, cos01_third)
+        for part, made, op in ((RE, im_sin2, SUBTRACT), (IM, im_cos2, ADD)):
+            nc.vector.tensor_tensor(out2[:, part, :], partly2[:, part, :], made[:], op)
+            for half, queue in ((0, nc.sync), (1, nc.scalar)):
+                queue.dma_start(stores[2, half, :, part, :], out2[half::2, part, :])

@@ -85,7 +85,8 @@ def tile_metapathaggrnet_kernel(tc, table, w, b, theta0, theta1, offs, out):
         nc.scalar.mul(sin01_third[:], sin01[:], 1.0 / 3.0)
 
         def project(node, part):
-            bank = banks.tile([D, HALF], F32, name="node%d_part%d" % (node, part))
+            tag = "node0_part%d" % part if node == 0 else "node12_part%d" % part
+            bank = banks.tile([D, HALF], F32, name="node%d_part%d" % (node, part), tag=tag)
             for half in (0, 1):
                 first = (2 * node + half) * COLS
                 picked = table_sb[:].indirect(offsets[:, first : first + COLS])
@@ -122,7 +123,7 @@ def tile_metapathaggrnet_kernel(tc, table, w, b, theta0, theta1, offs, out):
         nc.vector.tensor_tensor(turned1[:, RE, :], re_cos1[:], im_sin1[:], SUBTRACT)
         nc.vector.tensor_tensor(turned1[:, IM, :], re_sin1[:], im_cos1[:], ADD)
         for part in (RE, IM):
-            nc.vector.tensor_tensor(h1[:, part, :], out0[:, part, :], turned1[:, part, :], ADD)
+            nc.vector.scalar_tensor_tensor(h1[:, part, :], node0[part][:], bias[part], turned1[:, part, :], ADD, ADD)
             nc.scalar.mul(out1[:, part, :], h1[:, part, :], 1.0 / 2.0)
         for half in (0, 1):
             nc.sync.dma_start(stores[1, half], out1[half::2])

@@ -10,8 +10,8 @@ U16 = mybir.dt.uint16
 ADD = mybir.AluOpType.add
 SUBTRACT = mybir.AluOpType.subtract
 MULT = mybir.AluOpType.mult
-MAX = mybir.AluOpType.max
 SIN = mybir.ActivationFunctionType.Sin
+ABS = mybir.ActivationFunctionType.Abs
 IDENTITY = mybir.ActivationFunctionType.Identity
 
 D = 128
@@ -50,9 +50,9 @@ def tile_metapathaggrnet_kernel(tc, table, w, b, theta0, theta1, offs, out):
         first_sin = f32_tile("first_sin", 1)
         nc.scalar.activation(first_sin[:], half_pi[:], SIN)
         angle0 = f32_tile("angle0")
-        nc.scalar.dma_start(angle0[:], theta0.rearrange("k (h p) -> (k h) p", h=2))
+        nc.sync.dma_start(angle0[:], theta0.rearrange("k (h p) -> (k h) p", h=2))
         angle1 = f32_tile("angle1")
-        nc.scalar.dma_start(angle1[:], theta1.rearrange("k (h p) -> (k h) p", h=2))
+        nc.sync.dma_start(angle1[:], theta1.rearrange("k (h p) -> (k h) p", h=2))
 
         b_twice = held.tile([D, 2, 16, 2], F32, name="b_twice", align_bytes=64)
         nc.vector.tensor_copy(b_twice[:], b_raw[:].unsqueeze(3).to_broadcast([D, 2, 16, 2]))
@@ -73,16 +73,14 @@ def tile_metapathaggrnet_kernel(tc, table, w, b, theta0, theta1, offs, out):
         nc.scalar.activation(sin0[:], angle0[:], SIN)
         angle01 = f32_tile("angle01")
         nc.vector.tensor_tensor(angle01[:], angle0[:], angle1[:], ADD)
-        abs01 = f32_tile("abs01")
-        nc.vector.scalar_tensor_tensor(abs01[:], angle01[:], -1.0, angle01[:], MULT, MAX)
+        angles_work = held.tile([D, 2, HALF], F32, name="angles_work", tag="angles_work_then_out0")
+        abs01, sin01 = angles_work[:, 0, :], angles_work[:, 1, :]
+        nc.scalar.activation(abs01, angle01[:], ABS)
         cos01 = f32_tile("cos01")
-        sin01 = f32_tile("sin01")
-        nc.scalar.activation(sin01[:], angle01[:], SIN)
-        nc.scalar.activation(cos01[:], abs01[:], SIN, scale=-1.0, bias=half_pi[:, 0:1])
-        cos01_third = f32_tile("cos01_third")
+        nc.scalar.activation(sin01, angle01[:], SIN)
+        nc.scalar.activation(cos01[:], abs01, SIN, scale=-1.0, bias=half_pi[:, 0:1])
         sin01_third = f32_tile("sin01_third")
-        nc.scalar.mul(cos01_third[:], cos01[:], 1.0 / 3.0)
-        nc.scalar.mul(sin01_third[:], sin01[:], 1.0 / 3.0)
+        nc.scalar.mul(sin01_third[:], sin01, 1.0 / 3.0)
 
         def project(node, part):
             tag = "node0_part%d" % part if node == 0 else "node12_part%d" % part
@@ -103,18 +101,13 @@ def tile_metapathaggrnet_kernel(tc, table, w, b, theta0, theta1, offs, out):
             nc.vector.scalar_tensor_tensor(tile[:], bank[part][:], bias[part], factor[:], ADD, MULT)
             return tile
 
-        out0 = held.tile([D, 2, HALF], F32, name="out0")
+        out0 = held.tile([D, 2, HALF], F32, name="out0", tag="angles_work_then_out0")
         turned1 = held.tile([D, 2, HALF], F32, name="turned1")
         h1 = held.tile([D, 2, HALF], F32, name="h1")
         out1 = held.tile([D, 2, HALF], F32, name="out1")
         partly2 = held.tile([D, 2, HALF], F32, name="partly2")
         out2 = held.tile([D, 2, HALF], F32, name="out2")
         stores = out.rearrange("(r k) (s h p) -> s h k r p", r=2, s=3, h=2)
-
-        for part in (RE, IM):
-            nc.scalar.activation(out0[:, part, :], node0[part][:], IDENTITY, bias=bias[part])
-        for half in (0, 1):
-            nc.sync.dma_start(stores[0, half], out0[half::2])
 
         re_cos1 = product("re_cos1", node1, RE, cos0)
         re_sin1 = product("re_sin1", node1, RE, sin0)
@@ -124,17 +117,21 @@ def tile_metapathaggrnet_kernel(tc, table, w, b, theta0, theta1, offs, out):
         nc.vector.tensor_tensor(turned1[:, IM, :], re_sin1[:], im_cos1[:], ADD)
         for part in (RE, IM):
             nc.vector.scalar_tensor_tensor(h1[:, part, :], node0[part][:], bias[part], turned1[:, part, :], ADD, ADD)
+            nc.scalar.activation(out0[:, part, :], node0[part][:], IDENTITY, bias=bias[part])
+        for half in (0, 1):
+            nc.sync.dma_start(stores[0, half], out0[half::2])
+        for part in (RE, IM):
             nc.scalar.mul(out1[:, part, :], h1[:, part, :], 1.0 / 2.0)
         for half in (0, 1):
             nc.sync.dma_start(stores[1, half], out1[half::2])
 
-        re_cos2 = product("re_cos2", node2, RE, cos01_third)
+        re_cos2 = product("re_cos2", node2, RE, cos01)
         re_sin2 = product("re_sin2", node2, RE, sin01_third)
-        for part, made in ((RE, re_cos2), (IM, re_sin2)):
-            nc.vector.scalar_tensor_tensor(partly2[:, part, :], h1[:, part, :], 1.0 / 3.0, made[:], MULT, ADD)
+        nc.vector.tensor_tensor(partly2[:, RE, :], h1[:, RE, :], re_cos2[:], ADD)
+        im_cos2 = product("im_cos2", node2, IM, cos01)
         im_sin2 = product("im_sin2", node2, IM, sin01_third)
-        im_cos2 = product("im_cos2", node2, IM, cos01_third)
-        for part, made, op in ((RE, im_sin2, SUBTRACT), (IM, im_cos2, ADD)):
-            nc.vector.tensor_tensor(out2[:, part, :], partly2[:, part, :], made[:], op)
+        nc.vector.tensor_tensor(partly2[:, IM, :], h1[:, IM, :], im_cos2[:], ADD)
+        for part, made, op in ((RE, im_sin2, SUBTRACT), (IM, re_sin2, ADD)):
+            nc.vector.scalar_tensor_tensor(out2[:, part, :], partly2[:, part, :], 1.0 / 3.0, made[:], MULT, op)
             for half, queue in ((0, nc.sync), (1, nc.scalar)):
                 queue.dma_start(stores[2, half, :, part, :], out2[half::2, part, :])

@@ -41,10 +41,10 @@ def tile_metapathaggrnet_kernel(tc, table, w, b, theta0, theta1, offs, out):
         nc.gpsimd.memset(w_spread[:], 0.0)
 
         w_sb = held.tile([D, D], BF16, name="w_sb")
-        nc.sync.dma_start(w_sb[:], w)
+        nc.scalar.dma_start(w_sb[:], w)
         offsets = held.tile([D, 6 * COLS], U16, name="offsets")
         nc.sync.dma_start(offsets[:], offs)
-        nc.sync.dma_start(b_raw[::32], b.rearrange("(r g i) o -> g r (i o)", r=2, g=4))
+        nc.scalar.dma_start(b_raw[::32], b.rearrange("(r g i) o -> g r (i o)", r=2, g=4))
         table_sb = held.tile([D, S], BF16, name="table_sb")
         nc.sync.dma_start(table_sb[:], table)
         first_sin = f32_tile("first_sin", 1)
@@ -120,8 +120,7 @@ def tile_metapathaggrnet_kernel(tc, table, w, b, theta0, theta1, offs, out):
             nc.scalar.activation(out0[:, part, :], node0[part][:], IDENTITY, bias=bias[part])
         for half in (0, 1):
             nc.sync.dma_start(stores[0, half], out0[half::2])
-        for part in (RE, IM):
-            nc.scalar.mul(out1[:, part, :], h1[:, part, :], 1.0 / 2.0)
+        nc.scalar.mul(out1[:], h1[:], 1.0 / 2.0)
         for half in (0, 1):
             nc.sync.dma_start(stores[1, half], out1[half::2])
 

@@ -21,7 +21,6 @@ P = 512
 HALF = P // 2
 COLS = HALF // 16
 RE, IM = 0, 1
-WARM_UP_MATMULS = 4
 
 
 def tile_metapathaggrnet_kernel(tc, table, w, b, theta0, theta1, offs, out):
@@ -33,8 +32,6 @@ def tile_metapathaggrnet_kernel(tc, table, w, b, theta0, theta1, offs, out):
 
         half_pi = f32_tile("half_pi", 1)
         nc.vector.memset(half_pi[:], math.pi / 2)
-        zeros = held.tile([D, P], BF16, name="zeros")
-        nc.vector.memset(zeros[:], 0.0)
         b_raw = held.tile([D, 2, 16], F32, name="b_raw")
         nc.gpsimd.memset(b_raw[:], 0.0)
         w_spread = held.tile([D, 2, 2, K, 2], BF16, name="w_spread")
@@ -60,10 +57,6 @@ def tile_metapathaggrnet_kernel(tc, table, w, b, theta0, theta1, offs, out):
         for part in (RE, IM):
             nc.vector.transpose(bias_sb[:, part, :], b_twice[:, part].rearrange("q i j -> q (i j)"))
         bias = [bias_sb[:, part, 0:1] for part in (RE, IM)]
-
-        idle_bank = banks.tile([D, P], F32, name="idle_bank")
-        for step in range(WARM_UP_MATMULS):
-            nc.tensor.matmul(idle_bank[:], zeros[:, 0:D], zeros[:], start=True, stop=True)
 
         for half in (0, 1):
             nc.scalar.copy(w_spread[:, :, half, :, half], w_sb[:].rearrange("d (r k) -> d r k", r=2))

@@ -41,9 +41,10 @@ def tile_metapathaggrnet_kernel(tc, table, w, b, theta0, theta1, offs, out):
         nc.scalar.dma_start(w_sb[:], w)
         offsets = held.tile([D, 6 * COLS], U16, name="offsets")
         nc.sync.dma_start(offsets[:], offs)
-        nc.scalar.dma_start(b_raw[::32], b.rearrange("(r g i) o -> g r (i o)", r=2, g=4))
         table_sb = held.tile([D, S], BF16, name="table_sb")
-        nc.sync.dma_start(table_sb[:], table)
+        nc.sync.dma_start(table_sb[:, 0 : S // 2], table[:, 0 : S // 2])
+        nc.scalar.dma_start(table_sb[:, S // 2 : S], table[:, S // 2 : S])
+        nc.scalar.dma_start(b_raw[::32], b.rearrange("(r g i) o -> g r (i o)", r=2, g=4))
         first_sin = f32_tile("first_sin", 1)
         nc.scalar.activation(first_sin[:], half_pi[:], SIN)
         angle0 = f32_tile("angle0")

@@ -65,19 +65,16 @@ def tile_metapathaggrnet_kernel(tc, table, w, b, theta0, theta1, offs, out):
         nc.scalar.activation(cos0[:], angle0[:], SIN, bias=half_pi[:, 0:1])
         sin0 = f32_tile("sin0")
         nc.scalar.activation(sin0[:], angle0[:], SIN)
-        angle01 = f32_tile("angle01")
-        nc.vector.tensor_tensor(angle01[:], angle0[:], angle1[:], ADD)
         angles_work = held.tile([D, 2, HALF], F32, name="angles_work", tag="angles_work_then_out0")
-        abs01, sin01 = angles_work[:, 0, :], angles_work[:, 1, :]
-        nc.scalar.activation(abs01, angle01[:], ABS)
+        angle01, abs01 = angles_work[:, 0, :], angles_work[:, 1, :]
+        nc.vector.tensor_tensor(angle01, angle0[:], angle1[:], ADD)
+        nc.scalar.activation(abs01, angle01, ABS)
         cos01 = f32_tile("cos01")
-        nc.scalar.activation(sin01, angle01[:], SIN)
+        sin01 = f32_tile("sin01")
+        nc.scalar.activation(sin01[:], angle01, SIN)
         nc.scalar.activation(cos01[:], abs01, SIN, scale=-1.0, bias=half_pi[:, 0:1])
-        sin01_third = f32_tile("sin01_third")
-        nc.scalar.mul(sin01_third[:], sin01, 1.0 / 3.0)
 
-        def project(node, part):
-            tag = "node0_part%d" % part if node == 0 else "node12_part%d" % part
+        def project(node, part, tag):
             bank = banks.tile([D, HALF], F32, name="node%d_part%d" % (node, part), tag=tag)
             for half in (0, 1):
                 first = (2 * node + half) * COLS
@@ -86,45 +83,51 @@ def tile_metapathaggrnet_kernel(tc, table, w, b, theta0, theta1, offs, out):
                 nc.tensor.matmul(bank[:], weights, picked, start=(half == 0), stop=(half == 1))
             return bank
 
-        node1 = [project(1, part) for part in (RE, IM)]
-        node0 = [project(0, part) for part in (RE, IM)]
-        node2 = [project(2, part) for part in (RE, IM)]
+        node1 = [project(1, RE, "node12_re"), project(1, IM, "node1_im")]
+        node0 = [project(0, RE, "node0_re_then_2_im"), project(0, IM, "node0_im")]
+        node2 = [project(2, RE, "node12_re"), project(2, IM, "node0_re_then_2_im")]
 
-        def product(name, bank, part, factor):
-            tile = f32_tile(name)
+        def product(name, bank, part, factor, tag=None):
+            tile = held.tile([D, HALF], F32, name=name, tag=tag or name)
             nc.vector.scalar_tensor_tensor(tile[:], bank[part][:], bias[part], factor[:], ADD, MULT)
             return tile
 
         out0 = held.tile([D, 2, HALF], F32, name="out0", tag="angles_work_then_out0")
-        turned1 = held.tile([D, 2, HALF], F32, name="turned1")
+        turned1 = [held.tile([D, HALF], F32, name="turned1_" + tag, tag=tag) for tag in ("turned_re", "turned_im")]
         h1 = held.tile([D, 2, HALF], F32, name="h1")
         out1 = held.tile([D, 2, HALF], F32, name="out1")
         partly2 = held.tile([D, 2, HALF], F32, name="partly2")
         out2 = held.tile([D, 2, HALF], F32, name="out2")
         stores = out.rearrange("(r k) (s h p) -> s h k r p", r=2, s=3, h=2)
 
+        for part in (RE, IM):
+            nc.scalar.activation(out0[:, part, :], node0[part][:], IDENTITY, bias=bias[part])
+        for half in (0, 1):
+            nc.sync.dma_start(stores[0, half], out0[half::2])
+        cos01_third = f32_tile("cos01_third")
+        sin01_third = f32_tile("sin01_third")
+        nc.scalar.mul(sin01_third[:], sin01[:], 1.0 / 3.0)
+        nc.scalar.mul(cos01_third[:], cos01[:], 1.0 / 3.0)
+
         re_cos1 = product("re_cos1", node1, RE, cos0)
         re_sin1 = product("re_sin1", node1, RE, sin0)
         im_sin1 = product("im_sin1", node1, IM, sin0)
         im_cos1 = product("im_cos1", node1, IM, cos0)
-        nc.vector.tensor_tensor(turned1[:, RE, :], re_cos1[:], im_sin1[:], SUBTRACT)
-        nc.vector.tensor_tensor(turned1[:, IM, :], re_sin1[:], im_cos1[:], ADD)
+        nc.vector.tensor_tensor(turned1[RE][:], re_cos1[:], im_sin1[:], SUBTRACT)
+        nc.vector.tensor_tensor(turned1[IM][:], re_sin1[:], im_cos1[:], ADD)
         for part in (RE, IM):
-            nc.vector.scalar_tensor_tensor(h1[:, part, :], node0[part][:], bias[part], turned1[:, part, :], ADD, ADD)
-            nc.scalar.activation(out0[:, part, :], node0[part][:], IDENTITY, bias=bias[part])
-        for half in (0, 1):
-            nc.sync.dma_start(stores[0, half], out0[half::2])
+            nc.vector.tensor_tensor(h1[:, part, :], out0[:, part, :], turned1[part][:], ADD)
         nc.scalar.mul(out1[:], h1[:], 1.0 / 2.0)
         for half in (0, 1):
             nc.sync.dma_start(stores[1, half], out1[half::2])
 
-        re_cos2 = product("re_cos2", node2, RE, cos01)
-        re_sin2 = product("re_sin2", node2, RE, sin01_third)
-        nc.vector.tensor_tensor(partly2[:, RE, :], h1[:, RE, :], re_cos2[:], ADD)
-        im_cos2 = product("im_cos2", node2, IM, cos01)
+        re_cos2 = product("re_cos2", node2, RE, cos01, tag="turned_re")
+        re_sin2 = product("re_sin2", node2, RE, sin01, tag="turned_im")
+        for part, made in ((RE, re_cos2), (IM, re_sin2)):
+            nc.vector.tensor_tensor(partly2[:, part, :], h1[:, part, :], made[:], ADD)
         im_sin2 = product("im_sin2", node2, IM, sin01_third)
-        nc.vector.tensor_tensor(partly2[:, IM, :], h1[:, IM, :], im_cos2[:], ADD)
-        for part, made, op in ((RE, im_sin2, SUBTRACT), (IM, re_sin2, ADD)):
+        im_cos2 = product("im_cos2", node2, IM, cos01_third)
+        for part, made, op in ((RE, im_sin2, SUBTRACT), (IM, im_cos2, ADD)):
             nc.vector.scalar_tensor_tensor(out2[:, part, :], partly2[:, part, :], 1.0 / 3.0, made[:], MULT, op)
             for half, queue in ((0, nc.sync), (1, nc.scalar)):
                 queue.dma_start(stores[2, half, :, part, :], out2[half::2, part, :])

import math

import concourse.mybir as mybir

FLOPS = 2 * 128 * 128 * 1536

F32 = mybir.dt.float32
BF16 = mybir.dt.bfloat16
U16 = mybir.dt.uint16
ADD = mybir.AluOpType.add
SUBTRACT = mybir.AluOpType.subtract
MULT = mybir.AluOpType.mult
SIN = mybir.ActivationFunctionType.Sin
ABS = mybir.ActivationFunctionType.Abs
IDENTITY = mybir.ActivationFunctionType.Identity

D = 128
K = 64
S = 2048
P = 512
HALF = P // 2
COLS = HALF // 16
RE, IM = 0, 1


def tile_metapathaggrnet_kernel(tc, table, w, b, theta0, theta1, offs, out):
    nc = tc.nc
    with tc.tile_pool(name="held", bufs=1) as held, tc.psum_pool(name="banks", bufs=1) as banks:

        def f32_tile(name, cols=HALF):
            return held.tile([D, cols], F32, name=name)

        half_pi = f32_tile("half_pi", 1)
        nc.vector.memset(half_pi[:], math.pi / 2)
        b_raw = held.tile([D, 2, 16], F32, name="b_raw")
        nc.gpsimd.memset(b_raw[:], 0.0)
        w_spread = held.tile([D, 2, 2, K, 2], BF16, name="w_spread")
        nc.gpsimd.memset(w_spread[:], 0.0)

        w_sb = held.tile([D, D], BF16, name="w_sb")
        nc.scalar.dma_start(w_sb[:], w)
        offsets = held.tile([D, 6 * COLS], U16, name="offsets")
        nc.sync.dma_start(offsets[:], offs)
        table_sb = held.tile([D, S], BF16, name="table_sb")
        nc.sync.dma_start(table_sb[:, 0 : S // 2], table[:, 0 : S // 2])
        nc.scalar.dma_start(table_sb[:, S // 2 : S], table[:, S // 2 : S])
        nc.scalar.dma_start(b_raw[::32], b.rearrange("(r g i) o -> g r (i o)", r=2, g=4))
        first_sin = f32_tile("first_sin", 1)
        nc.scalar.activation(first_sin[:], half_pi[:], SIN)
        angle0 = f32_tile("angle0")
        nc.sync.dma_start(angle0[:], theta0.rearrange("k (h p) -> (k h) p", h=2))
        angle1 = f32_tile("angle1")
        nc.sync.dma_start(angle1[:], theta1.rearrange("k (h p) -> (k h) p", h=2))

        b_twice = held.tile([D, 2, 16, 2], F32, name="b_twice", align_bytes=64)
        nc.vector.tensor_copy(b_twice[:], b_raw[:].unsqueeze(3).to_broadcast([D, 2, 16, 2]))
        bias_sb = held.tile([D, 2, 32], F32, name="bias_sb", align_bytes=64)
        for part in (RE, IM):
            nc.vector.transpose(bias_sb[:, part, :], b_twice[:, part].rearrange("q i j -> q (i j)"))
        bias = [bias_sb[:, part, 0:1] for part in (RE, IM)]

        for half in (0, 1):
            nc.scalar.copy(w_spread[:, :, half, :, half], w_sb[:].rearrange("d (r k) -> d r k", r=2))
        cos0 = f32_tile("cos0")
        nc.scalar.activation(cos0[:], angle0[:], SIN, bias=half_pi[:, 0:1])
        sin0 = f32_tile("sin0")
        nc.scalar.activation(sin0[:], angle0[:], SIN)
        angles_work = held.tile([D, 2, HALF], F32, name="angles_work", tag="angles_work_then_out0")
        angle01, abs01 = angles_work[:, 0, :], angles_work[:, 1, :]
        nc.vector.tensor_tensor(angle01, angle0[:], angle1[:], ADD)
        nc.scalar.activation(abs01, angle01, ABS)
        cos01 = f32_tile("cos01")
        sin01 = f32_tile("sin01")
        nc.scalar.activation(sin01[:], angle01, SIN)
        nc.scalar.activation(cos01[:], abs01, SIN, scale=-1.0, bias=half_pi[:, 0:1])

        def project(node, part, tag):
            bank = banks.tile([D, HALF], F32, name="node%d_part%d" % (node, part), tag=tag)
            for half in (0, 1):
                first = (2 * node + half) * COLS
                picked = table_sb[:].indirect(offsets[:, first : first + COLS])
                weights = w_spread[:, part, half].rearrange("d k j -> d (k j)")
                nc.tensor.matmul(bank[:], weights, picked, start=(half == 0), stop=(half == 1))
            return bank

        node1 = [project(1, RE, "node12_re"), project(1, IM, "node1_im")]
        node0 = [project(0, RE, "node0_re_then_2_im"), project(0, IM, "node0_im")]
        node2 = [project(2, RE, "node12_re"), project(2, IM, "node0_re_then_2_im")]

        def product(name, bank, part, factor, tag=None):
            tile = held.tile([D, HALF], F32, name=name, tag=tag or name)
            nc.vector.scalar_tensor_tensor(tile[:], bank[part][:], bias[part], factor[:], ADD, MULT)
            return tile

        out0 = held.tile([D, 2, HALF], F32, name="out0", tag="angles_work_then_out0")
        turned1 = [held.tile([D, HALF], F32, name="turned1_" + tag, tag=tag) for tag in ("turned_re", "turned_im")]
        h1 = held.tile([D, 2, HALF], F32, name="h1")
        out1 = held.tile([D, 2, HALF], F32, name="out1")
        partly2 = held.tile([D, 2, HALF], F32, name="partly2")
        out2 = held.tile([D, 2, HALF], F32, name="out2")
        stores = out.rearrange("(r k) (s h p) -> s h k r p", r=2, s=3, h=2)

        for part in (RE, IM):
            nc.scalar.activation(out0[:, part, :], node0[part][:], IDENTITY, bias=bias[part])
        for half in (0, 1):
            nc.sync.dma_start(stores[0, half], out0[half::2])
        cos01_third = f32_tile("cos01_third")
        sin01_third = f32_tile("sin01_third")
        nc.scalar.mul(sin01_third[:], sin01[:], 1.0 / 3.0)
        nc.scalar.mul(cos01_third[:], cos01[:], 1.0 / 3.0)

        re_cos1 = product("re_cos1", node1, RE, cos0)
        re_sin1 = product("re_sin1", node1, RE, sin0)
        im_sin1 = product("im_sin1", node1, IM, sin0)
        im_cos1 = product("im_cos1", node1, IM, cos0)
        nc.vector.tensor_tensor(turned1[RE][:], re_cos1[:], im_sin1[:], SUBTRACT)
        nc.vector.tensor_tensor(turned1[IM][:], re_sin1[:], im_cos1[:], ADD)
        for part in (RE, IM):
            nc.vector.tensor_tensor(h1[:, part, :], out0[:, part, :], turned1[part][:], ADD)
        nc.scalar.mul(out1[:], h1[:], 1.0 / 2.0)
        for half in (0, 1):
            nc.sync.dma_start(stores[1, half], out1[half::2])

        re_cos2 = product("re_cos2", node2, RE, cos01, tag="turned_re")
        re_sin2 = product("re_sin2", node2, RE, sin01, tag="turned_im")
        for part, made in ((RE, re_cos2), (IM, re_sin2)):
            nc.vector.tensor_tensor(partly2[:, part, :], h1[:, part, :], made[:], ADD)
        im_sin2 = product("im_sin2", node2, IM, sin01_third)
        im_cos2 = product("im_cos2", node2, IM, cos01_third)
        for part, made, op in ((RE, im_sin2, SUBTRACT), (IM, im_cos2, ADD)):
            nc.vector.scalar_tensor_tensor(out2[:, part, :], partly2[:, part, :], 1.0 / 3.0, made[:], MULT, op)
            for half, queue in ((0, nc.sync), (1, nc.scalar)):
                queue.dma_start(stores[2, half, :, part, :], out2[half::2, part, :])
